import numpy as np
import ml_dtypes


def mxq(x, axis, fmt="e4m3"):
    dtype, down = {"e4m3": (ml_dtypes.float8_e4m3fn, 7), "e5m2": (ml_dtypes.float8_e5m2, 14)}[fmt]
    v = np.moveaxis(np.asarray(x, np.float32).astype(ml_dtypes.bfloat16).astype(np.float64), axis, -1)
    blocks = v.reshape(v.shape[:-1] + (-1, 32))
    amax = np.abs(blocks).max(-1, keepdims=True)
    byte = np.maximum(np.where(amax > 0, np.frexp(amax)[1] - 1 + 127, 0) - down, 1)
    scale = np.exp2(byte - 127.0)
    codes = (blocks / scale).astype(np.float32).astype(dtype).astype(np.float64)
    return np.moveaxis((codes * scale).reshape(v.shape), -1, axis)


WIDE = False


def mx_kscale(k):
    if not WIDE:
        return np.ones(k)
    levels = np.array([10, -10, 5, -5, 0])
    if k % 512:
        return np.exp2(np.random.permutation(np.resize(levels, k // 32))).repeat(32)
    a = np.empty((k // 512, 16))
    for p in range(k // 512):
        a[p, :8] = np.random.permutation(np.resize(levels, 8))
        for g in range(8):
            far = levels[np.abs(levels - a[p, g]) >= 10]
            a[p, g + 8] = far[np.random.randint(len(far))]
    return np.exp2(a.ravel()).repeat(32)


BF16 = ml_dtypes.bfloat16


def bf(x):
    return np.asarray(x, np.float32).astype(BF16)


def f64(x):
    return np.asarray(x).astype(np.float64)


B, N, D_IN, H, D_HEAD, D_EXPAND = 2, 512, 512, 8, 128, 2048
D_Q = D_HEAD * H
D_V = D_IN * H
D_QKV = 2 * D_Q + D_V
EPS = 1e-5


def feature_norm(x, gamma, beta):
    mean = x.mean(axis=1, keepdims=True)
    var = x.var(axis=1, keepdims=True)
    return gamma * (x - mean) / np.sqrt(var + EPS) + beta


def sigmoid(v):
    e = np.exp(-np.abs(v))
    return np.where(v >= 0.0, 1.0, e) / (1.0 + e)


def swish(v):
    return v * sigmoid(v)


def setup_inputs():
    wcol = np.concatenate([np.full(2 * D_Q, 1.9 / np.sqrt(D_HEAD * D_IN)), np.full(D_V, 0.5 / np.sqrt(D_IN))])
    bcol = np.concatenate([np.full(2 * D_Q, 0.03), np.full(D_V, 0.1)])
    s = mx_kscale(D_IN)
    t = s / s.min()
    return {"x": bf(1.5 * np.random.standard_normal((B, N, D_IN)) + 0.5 * np.random.standard_normal((1, 1, D_IN))),
            "pos_enc": bf(np.random.standard_normal((1, N, D_IN)) * t),
            "gamma1": bf((1.0 + 0.1 * np.random.standard_normal((1, 1, D_IN))) * t),
            "beta1": bf(0.1 * np.random.standard_normal((1, 1, D_IN)) * t),
            "W_qkv": bf(np.random.standard_normal((D_IN, D_QKV)) * wcol / t[:, None]),
            "b_qkv": bf(np.random.standard_normal(D_QKV) * bcol)}


def reference(x, pos_enc, gamma1, beta1, W_qkv, b_qkv):
    h = feature_norm(f64(x), f64(gamma1), f64(beta1)) + f64(pos_enc)
    a = swish(h)
    return (mxq(a, 2, "e4m3") @ mxq(f64(W_qkv), 0, "e4m3")) + f64(b_qkv)

@@ -1,0 +1,245 @@
+from contextlib import ExitStack
+
+import concourse.mybir as mybir
+from concourse.masks import make_identity
+
+F32 = mybir.dt.float32
+BF16 = mybir.dt.bfloat16
+U32 = mybir.dt.uint32
+U8 = mybir.dt.uint8
+FP8X4 = mybir.dt.float8_e4m3fn_x4
+ALU = mybir.AluOpType
+ACT = mybir.ActivationFunctionType
+
+P = 128
+PACK = 4
+BATCH, TOKENS, D_IN, D_OUT = 2, 512, 512, 6144
+EPS = 1e-5
+TOKEN_TILES = TOKENS // P
+UNITS = BATCH * TOKEN_TILES
+N_PASS = 512
+HALF = N_PASS // 2
+PASSES_PER_STORE = 3
+GROUP = N_PASS * PASSES_PER_STORE
+N_GROUPS = D_OUT // GROUP
+SCALAR_SHARE = 3
+RUN = 4
+
+FLOPS = 2 * BATCH * TOKENS * D_IN * D_OUT
+
+
+def regroup(copy, grouped, planes):
+    copy(
+        out=grouped.rearrange("p (c i) t -> p c t i", i=RUN),
+        in_=planes.rearrange("p t (c i) -> p c t i", i=RUN),
+    )
+
+
+def tile_attentionblock_pa_kernel(tc, x, pos_enc, gamma1, beta1, W_qkv, b_qkv, out):
+    nc = tc.nc
+    with ExitStack() as ctx:
+        ctx.enter_context(tc.manual_schedule())
+        keep = ctx.enter_context(tc.tile_pool(name="keep", bufs=1))
+        w_stage = ctx.enter_context(tc.tile_pool(name="w_stage", bufs=4))
+        out_stage = ctx.enter_context(tc.tile_pool(name="out_stage", bufs=8))
+
+        one = keep.tile([P, 1], F32)
+        nc.vector.memset(one[:], 1.0)
+        ident = keep.tile([P, P], F32)
+        make_identity(nc, ident[:])
+        warm = keep.tile([P, 2], F32)
+        nc.scalar.activation(out=warm[:, 0:1], in_=one[:], func=ACT.Sqrt)
+
+        gamma_sb = keep.tile([P, PACK], BF16)
+        beta_sb = keep.tile([P, PACK], BF16)
+        x_sb = [keep.tile([P, TOKEN_TILES, D_IN], BF16, name="x_sb%d" % b) for b in range(BATCH)]
+        pos_sb = keep.tile([P, TOKEN_TILES, D_IN], BF16)
+        w_raw = [keep.tile([P, PACK, GROUP], BF16, name="w_raw%d" % g) for g in range(N_GROUPS)]
+        bias_sb = keep.tile([P, D_OUT], BF16)
+        w_planes = W_qkv.rearrange("(p t) n -> p t n", t=PACK)
+
+        def load_x(b):
+            nc.sync.dma_start(out=x_sb[b][:], in_=x[b].rearrange("(m i) d -> m i d", i=TOKEN_TILES))
+
+        def load_w(g):
+            nc.sync.dma_start(out=w_raw[g][:], in_=w_planes[:, :, g * GROUP : (g + 1) * GROUP])
+
+        for b in range(BATCH):
+            load_x(b)
+        nc.sync.dma_start(out=gamma_sb[:], in_=gamma1.rearrange("a b (p t) -> (a b p) t", t=PACK))
+        nc.sync.dma_start(out=beta_sb[:], in_=beta1.rearrange("a b (p t) -> (a b p) t", t=PACK))
+        nc.sync.dma_start(out=pos_sb[:], in_=pos_enc[0].rearrange("(m i) d -> m i d", i=TOKEN_TILES))
+        load_w(0)
+        load_w(1)
+        nc.sync.dma_start(out=bias_sb[:], in_=b_qkv.partition_broadcast(P))
+        for g in range(2, N_GROUPS):
+            load_w(g)
+
+        w_codes = keep.tile([P, D_OUT], U32, align_bytes=64)
+        w_scales = keep.tile([P, D_OUT], U8, align_bytes=64)
+        w_grouped = {}
+
+        def regroup_w_half(c, half, copy):
+            g, j = divmod(c, PASSES_PER_STORE)
+            if half == 0:
+                w_grouped[c] = w_stage.tile([P, N_PASS, PACK], BF16, name="w_grouped", align_bytes=64)
+            first = half * HALF
+            regroup(
+                copy,
+                w_grouped[c][:, first : first + HALF, :],
+                w_raw[g][:, :, j * N_PASS + first : j * N_PASS + first + HALF],
+            )
+
+        def gpsimd_copy(out, in_):
+            nc.gpsimd.tensor_scalar(out=out, in0=in_, scalar1=1.0, scalar2=0.0, op0=ALU.mult, op1=ALU.add)
+
+        def quantise_w_chunk(c):
+            cols = slice(c * N_PASS, (c + 1) * N_PASS)
+            nc.vector.quantize_mx(
+                out=w_codes[:, cols].bitcast(FP8X4),
+                scales=w_scales[:, cols],
+                in_=w_grouped[c][:].rearrange("p n t -> p (n t)"),
+            )
+
+        xT = {}
+        posT_sb = keep.tile([P, PACK, TOKENS], BF16)
+        scale = keep.tile([P, BATCH, PACK], F32)
+        shift = keep.tile([P, BATCH, PACK], F32)
+        h_planes = [keep.tile([P, PACK, TOKENS], F32, name="h_planes%d" % b) for b in range(BATCH)]
+        a_planes = [keep.tile([P, PACK, TOKENS], BF16, name="a_planes%d" % b) for b in range(BATCH)]
+        a_grouped = [keep.tile([P, TOKENS, PACK], BF16, name="a_grouped%d" % b, align_bytes=64) for b in range(BATCH)]
+        a_codes = [keep.tile([P, TOKENS], U32, name="a_codes%d" % b, align_bytes=64) for b in range(BATCH)]
+        a_scales = [keep.tile([P, TOKENS], U8, name="a_scales%d" % b, align_bytes=64) for b in range(BATCH)]
+
+        def swish_plane(b, t):
+            nc.vector.scalar_tensor_tensor(
+                out=h_planes[b][:, t, :],
+                in0=plane(xT[b], t),
+                scalar=scale[:, b, t : t + 1],
+                in1=posT_sb[:, t, :],
+                op0=ALU.mult,
+                op1=ALU.add,
+            )
+            nc.scalar.activation(
+                out=a_planes[b][:, t, :],
+                in_=h_planes[b][:, t, :],
+                func=ACT.Silu,
+                bias=shift[:, b, t : t + 1],
+                scale=1.0,
+            )
+
+        def regroup_a(b):
+            regroup(nc.vector.tensor_copy, a_grouped[b][:], a_planes[b][:])
+
+        def quantise_a(b):
+            nc.vector.quantize_mx(
+                out=a_codes[b][:].bitcast(FP8X4),
+                scales=a_scales[b][:],
+                in_=a_grouped[b][:].rearrange("p n t -> p (n t)"),
+            )
+
+        stats = keep.tile([P, BATCH * PACK, 6], F32)
+        mean_var = keep.tile([P, BATCH * PACK, 2], F32)
+
+        def transpose_planes(rows_sb, name):
+            words = rows_sb[:].bitcast(F32)
+            banks = []
+            for h in range(PACK // 2):
+                bank = head_psum.tile([P, TOKENS], F32, name="%s_%d" % (name, h))
+                for i in range(TOKEN_TILES):
+                    nc.tensor.transpose(bank[:, i * P : (i + 1) * P], words[:, i, h :: PACK // 2], ident[:])
+                banks.append(bank)
+            return banks
+
+        def pair(bank):
+            return bank[:].bitcast(BF16).rearrange("p (n e) -> p e n", e=2)
+
+        def plane(banks, t):
+            return pair(banks[t // 2])[:, t % 2, :]
+
+        def statistics(b):
+            for t in range(PACK):
+                nc.vector.bn_stats(out=stats[:, b * PACK + t, :], in_=plane(xT[b], t))
+            for t in range(PACK):
+                nc.vector.bn_aggr(out=mean_var[:, b * PACK + t, :], in_=stats[:, b * PACK + t, :])
+
+        with tc.psum_pool(name="head_psum", bufs=1) as head_psum:
+            for b in range(BATCH):
+                xT[b] = transpose_planes(x_sb[b], "xT%d" % b)
+                statistics(b)
+            posT = transpose_planes(pos_sb, "posT")
+            for h in range(PACK // 2):
+                nc.scalar.copy(out=posT_sb[:, 2 * h : 2 * h + 2, :], in_=pair(posT[h]))
+            for half in range(2):
+                regroup_w_half(PASSES_PER_STORE - 1, half, gpsimd_copy)
+            for half in range(2):
+                regroup_w_half(0, half, nc.vector.tensor_copy)
+
+            std = keep.tile([P, BATCH, PACK], F32)
+            rstd = keep.tile([P, BATCH, PACK], F32)
+            mean_scale = keep.tile([P, BATCH, PACK], F32)
+            mean = mean_var[:, :, 0].rearrange("p (b t) -> p b t", b=BATCH)
+            var = mean_var[:, :, 1].rearrange("p (b t) -> p b t", b=BATCH)
+            gamma = gamma_sb[:].unsqueeze(1).to_broadcast([P, BATCH, PACK])
+            beta = beta_sb[:].unsqueeze(1).to_broadcast([P, BATCH, PACK])
+            nc.scalar.activation(out=std[:], in_=var, func=ACT.Sqrt, bias=EPS, scale=1.0)
+            nc.scalar.activation(out=warm[:, 1:2], in_=std[:, 0, 0:1], func=ACT.Silu)
+            nc.vector.reciprocal(out=rstd[:], in_=std[:])
+            nc.vector.tensor_tensor(out=scale[:], in0=rstd[:], in1=gamma, op=ALU.mult)
+            nc.vector.tensor_tensor(out=mean_scale[:], in0=mean, in1=scale[:], op=ALU.mult)
+            nc.vector.tensor_tensor(out=shift[:], in0=beta, in1=mean_scale[:], op=ALU.subtract)
+
+            for b in range(BATCH):
+                for t in range(PACK):
+                    swish_plane(b, t)
+                if b == 0:
+                    for c in range(1, PASSES_PER_STORE - 1):
+                        for half in range(2):
+                            regroup_w_half(c, half, nc.scalar.copy)
+
+        regroup_a(0)
+        quantise_w_chunk(0)
+        quantise_a(0)
+        quantise_w_chunk(PASSES_PER_STORE - 1)
+        for c in range(1, PASSES_PER_STORE - 1):
+            quantise_w_chunk(c)
+
+        acc_psum = ctx.enter_context(tc.psum_pool(name="acc_psum", bufs=8, reuse_waits="tile"))
+        for g in range(N_GROUPS):
+            for u in range(UNITS):
+                b, i = divmod(u, TOKEN_TILES)
+                tokens = slice(i * P, (i + 1) * P)
+                result = out_stage.tile([P, GROUP], F32)
+                for j in range(PASSES_PER_STORE):
+                    cols = slice(g * GROUP + j * N_PASS, g * GROUP + (j + 1) * N_PASS)
+                    acc = acc_psum.tile([P, N_PASS], F32)
+                    nc.tensor.matmul_mx(
+                        out=acc[:],
+                        lhsT=a_codes[b][:, tokens].bitcast(FP8X4),
+                        lhsT_scale=a_scales[b][:, tokens],
+                        rhs=w_codes[:, cols].bitcast(FP8X4),
+                        rhs_scale=w_scales[:, cols],
+                        start=True,
+                        stop=True,
+                    )
+                    part = result[:, j * N_PASS : (j + 1) * N_PASS]
+                    if ((g * UNITS + u) * PASSES_PER_STORE + j) % SCALAR_SHARE == 0:
+                        nc.scalar.copy(out=part, in_=acc[:])
+                        nc.gpsimd.tensor_tensor(out=part, in0=part, in1=bias_sb[:, cols], op=ALU.add)
+                    else:
+                        nc.vector.tensor_tensor(out=part, in0=acc[:], in1=bias_sb[:, cols], op=ALU.add)
+                nc.sync.dma_start(
+                    out=out[b].rearrange("(m i) n -> i m n", i=TOKEN_TILES)[i, :, g * GROUP : (g + 1) * GROUP],
+                    in_=result[:],
+                )
+                if g == 0 and b + 1 < BATCH:
+                    if i == 0:
+                        regroup_a(b + 1)
+                    if i == 1:
+                        quantise_a(b + 1)
+                if g + 1 < N_GROUPS:
+                    next_first = (g + 1) * PASSES_PER_STORE
+                    if u < 2 * PASSES_PER_STORE:
+                        regroup_w_half(next_first + u // 2, u % 2, nc.scalar.copy)
+                    if u >= 2 and u % 2 == 0:
+                        quantise_w_chunk(next_first + u // 2 - 1)

@@ -23,6 +23,10 @@ PASSES_PER_STORE = 3
 GROUP = N_PASS * PASSES_PER_STORE
 N_GROUPS = D_OUT // GROUP
 SCALAR_SHARE = 3
+BIAS_ROWS = 16
+BIAS_ROW = D_OUT // BIAS_ROWS
+BIAS_ROWS_PER_BANK = 2
+BIAS_BANKS_PER_GROUP = GROUP // (BIAS_ROWS_PER_BANK * BIAS_ROW)
 RUN = 4
 
 FLOPS = 2 * BATCH * TOKENS * D_IN * D_OUT
@@ -47,6 +51,10 @@ def tile_attentionblock_pa_kernel(tc, x, pos_enc, gamma1, beta1, W_qkv, b_qkv, o
         nc.vector.memset(one[:], 1.0)
         ident = keep.tile([P, P], F32)
         make_identity(nc, ident[:])
+        ident_bf = keep.tile([P, P], BF16)
+        bias_rows = keep.tile([P, BIAS_ROW], BF16)
+        nc.vector.memset(bias_rows[:], 0.0)
+        nc.vector.tensor_copy(out=ident_bf[:], in_=ident[:])
         warm = keep.tile([P, 2], F32)
         nc.scalar.activation(out=warm[:, 0:1], in_=one[:], func=ACT.Sqrt)
 
@@ -64,6 +72,7 @@ def tile_attentionblock_pa_kernel(tc, x, pos_enc, gamma1, beta1, W_qkv, b_qkv, o
         def load_w(g):
             nc.sync.dma_start(out=w_raw[g][:], in_=w_planes[:, :, g * GROUP : (g + 1) * GROUP])
 
+        nc.sync.dma_start(out=bias_rows[0:BIAS_ROWS, :], in_=b_qkv.rearrange("(r n) -> r n", n=BIAS_ROW))
         for b in range(BATCH):
             load_x(b)
         nc.sync.dma_start(out=gamma_sb[:], in_=gamma1.rearrange("a b (p t) -> (a b p) t", t=PACK))
@@ -71,7 +80,6 @@ def tile_attentionblock_pa_kernel(tc, x, pos_enc, gamma1, beta1, W_qkv, b_qkv, o
         nc.sync.dma_start(out=pos_sb[:], in_=pos_enc[0].rearrange("(m i) d -> m i d", i=TOKEN_TILES))
         load_w(0)
         load_w(1)
-        nc.sync.dma_start(out=bias_sb[:], in_=b_qkv.partition_broadcast(P))
         for g in range(2, N_GROUPS):
             load_w(g)
 
@@ -138,6 +146,20 @@ def tile_attentionblock_pa_kernel(tc, x, pos_enc, gamma1, beta1, W_qkv, b_qkv, o
                 in_=a_grouped[b][:].rearrange("p n t -> p (n t)"),
             )
 
+        def spread_bias_bank(k, psum, name, copy):
+            bank = psum.tile([P, 2 * N_PASS], BF16, name=name)
+            for r in range(BIAS_ROWS_PER_BANK):
+                row = k * BIAS_ROWS_PER_BANK + r
+                nc.tensor.matmul(
+                    bank[:, r * BIAS_ROW : (r + 1) * BIAS_ROW],
+                    lhsT=ident_bf[:, row : row + 1].to_broadcast([P, P]),
+                    rhs=bias_rows[:],
+                    start=True,
+                    stop=True,
+                )
+            width = BIAS_ROWS_PER_BANK * BIAS_ROW
+            copy(out=bias_sb[:, k * width : (k + 1) * width], in_=bank[:, 0:width])
+
         stats = keep.tile([P, BATCH * PACK, 6], F32)
         mean_var = keep.tile([P, BATCH * PACK, 2], F32)
 
@@ -164,6 +186,8 @@ def tile_attentionblock_pa_kernel(tc, x, pos_enc, gamma1, beta1, W_qkv, b_qkv, o
                 nc.vector.bn_aggr(out=mean_var[:, b * PACK + t, :], in_=stats[:, b * PACK + t, :])
 
         with tc.psum_pool(name="head_psum", bufs=1) as head_psum:
+            for k in range(BIAS_BANKS_PER_GROUP):
+                spread_bias_bank(k, head_psum, "bias_bank%d" % k, nc.vector.tensor_copy)
             for b in range(BATCH):
                 xT[b] = transpose_planes(x_sb[b], "xT%d" % b)
                 statistics(b)
@@ -237,6 +261,9 @@ def tile_attentionblock_pa_kernel(tc, x, pos_enc, gamma1, beta1, W_qkv, b_qkv, o
                         regroup_a(b + 1)
                     if i == 1:
                         quantise_a(b + 1)
+                if g + 1 < N_GROUPS and u >= UNITS - BIAS_BANKS_PER_GROUP:
+                    k = (g + 1) * BIAS_BANKS_PER_GROUP + u - (UNITS - BIAS_BANKS_PER_GROUP)
+                    spread_bias_bank(k, acc_psum, "acc", nc.scalar.copy)
                 if g + 1 < N_GROUPS:
                     next_first = (g + 1) * PASSES_PER_STORE
                     if u < 2 * PASSES_PER_STORE:

@@ -16,13 +16,13 @@ PACK = 4
 BATCH, TOKENS, D_IN, D_OUT = 2, 512, 512, 6144
 EPS = 1e-5
 TOKEN_TILES = TOKENS // P
-UNITS = BATCH * TOKEN_TILES
 N_PASS = 512
 HALF = N_PASS // 2
 PASSES_PER_STORE = 3
 GROUP = N_PASS * PASSES_PER_STORE
 N_GROUPS = D_OUT // GROUP
-SCALAR_SHARE = 3
+UNITS_PER_GROUP = BATCH * TOKEN_TILES
+HALF_TOKENS = TOKENS // 2
 BIAS_ROWS = 16
 BIAS_ROW = D_OUT // BIAS_ROWS
 BIAS_ROWS_PER_BANK = 2
@@ -46,42 +46,37 @@ def tile_attentionblock_pa_kernel(tc, x, pos_enc, gamma1, beta1, W_qkv, b_qkv, o
         keep = ctx.enter_context(tc.tile_pool(name="keep", bufs=1))
         w_stage = ctx.enter_context(tc.tile_pool(name="w_stage", bufs=4))
         out_stage = ctx.enter_context(tc.tile_pool(name="out_stage", bufs=8))
+        psum = ctx.enter_context(tc.psum_pool(name="psum", bufs=8, reuse_waits="tile"))
 
-        one = keep.tile([P, 1], F32)
-        nc.vector.memset(one[:], 1.0)
         ident = keep.tile([P, P], F32)
         make_identity(nc, ident[:])
-        ident_bf = keep.tile([P, P], BF16)
+        one = keep.tile([P, 1], F32)
+        nc.vector.memset(one[:], 1.0)
         bias_rows = keep.tile([P, BIAS_ROW], BF16)
         nc.vector.memset(bias_rows[:], 0.0)
+        ident_bf = keep.tile([P, P], BF16)
         nc.vector.tensor_copy(out=ident_bf[:], in_=ident[:])
         warm = keep.tile([P, 2], F32)
         nc.scalar.activation(out=warm[:, 0:1], in_=one[:], func=ACT.Sqrt)
 
-        gamma_sb = keep.tile([P, PACK], BF16)
-        beta_sb = keep.tile([P, PACK], BF16)
         x_sb = [keep.tile([P, TOKEN_TILES, D_IN], BF16, name="x_sb%d" % b) for b in range(BATCH)]
         pos_sb = keep.tile([P, TOKEN_TILES, D_IN], BF16)
+        gamma_sb = keep.tile([P, PACK], BF16)
+        beta_sb = keep.tile([P, PACK], BF16)
         w_raw = [keep.tile([P, PACK, GROUP], BF16, name="w_raw%d" % g) for g in range(N_GROUPS)]
-        bias_sb = keep.tile([P, D_OUT], BF16)
         w_planes = W_qkv.rearrange("(p t) n -> p t n", t=PACK)
 
-        def load_x(b):
-            nc.sync.dma_start(out=x_sb[b][:], in_=x[b].rearrange("(m i) d -> m i d", i=TOKEN_TILES))
+        def load_tokens(rows_sb, rows):
+            nc.sync.dma_start(out=rows_sb[:], in_=rows.rearrange("(m i) d -> m i d", i=TOKEN_TILES))
 
-        def load_w(g):
-            nc.sync.dma_start(out=w_raw[g][:], in_=w_planes[:, :, g * GROUP : (g + 1) * GROUP])
-
+        load_tokens(x_sb[0], x[0])
         nc.sync.dma_start(out=bias_rows[0:BIAS_ROWS, :], in_=b_qkv.rearrange("(r n) -> r n", n=BIAS_ROW))
-        for b in range(BATCH):
-            load_x(b)
         nc.sync.dma_start(out=gamma_sb[:], in_=gamma1.rearrange("a b (p t) -> (a b p) t", t=PACK))
         nc.sync.dma_start(out=beta_sb[:], in_=beta1.rearrange("a b (p t) -> (a b p) t", t=PACK))
-        nc.sync.dma_start(out=pos_sb[:], in_=pos_enc[0].rearrange("(m i) d -> m i d", i=TOKEN_TILES))
-        load_w(0)
-        load_w(1)
-        for g in range(2, N_GROUPS):
-            load_w(g)
+        load_tokens(x_sb[1], x[1])
+        load_tokens(pos_sb, pos_enc[0])
+        for g in range(N_GROUPS):
+            nc.sync.dma_start(out=w_raw[g][:], in_=w_planes[:, :, g * GROUP : (g + 1) * GROUP])
 
         w_codes = keep.tile([P, D_OUT], U32, align_bytes=64)
         w_scales = keep.tile([P, D_OUT], U8, align_bytes=64)
@@ -98,6 +93,25 @@ def tile_attentionblock_pa_kernel(tc, x, pos_enc, gamma1, beta1, W_qkv, b_qkv, o
                 w_raw[g][:, :, j * N_PASS + first : j * N_PASS + first + HALF],
             )
 
+        def interleave(grouped, planes):
+            bank = psum.tile([P, 2 * N_PASS], BF16, name="bank")
+            for q in range(2):
+                nc.tensor.matmul(
+                    bank[:, q * N_PASS : (q + 1) * N_PASS],
+                    lhsT=ident_bf[:],
+                    rhs=planes[:, :, q * P : (q + 1) * P].rearrange("p t n -> p n t"),
+                    start=True,
+                    stop=True,
+                )
+            nc.scalar.copy(out=grouped.rearrange("p n t -> p (n t)"), in_=bank[:])
+
+        def interleave_w_half(c, half):
+            g, j = divmod(c, PASSES_PER_STORE)
+            if half == 0:
+                w_grouped[c] = w_stage.tile([P, N_PASS, PACK], BF16, name="w_grouped", align_bytes=64)
+            first = j * N_PASS + half * HALF
+            interleave(w_grouped[c][:, half * HALF : (half + 1) * HALF, :], w_raw[g][:, :, first : first + HALF])
+
         def gpsimd_copy(out, in_):
             nc.gpsimd.tensor_scalar(out=out, in0=in_, scalar1=1.0, scalar2=0.0, op0=ALU.mult, op1=ALU.add)
 
@@ -109,45 +123,10 @@ def tile_attentionblock_pa_kernel(tc, x, pos_enc, gamma1, beta1, W_qkv, b_qkv, o
                 in_=w_grouped[c][:].rearrange("p n t -> p (n t)"),
             )
 
-        xT = {}
-        posT_sb = keep.tile([P, PACK, TOKENS], BF16)
-        scale = keep.tile([P, BATCH, PACK], F32)
-        shift = keep.tile([P, BATCH, PACK], F32)
-        h_planes = [keep.tile([P, PACK, TOKENS], F32, name="h_planes%d" % b) for b in range(BATCH)]
-        a_planes = [keep.tile([P, PACK, TOKENS], BF16, name="a_planes%d" % b) for b in range(BATCH)]
-        a_grouped = [keep.tile([P, TOKENS, PACK], BF16, name="a_grouped%d" % b, align_bytes=64) for b in range(BATCH)]
-        a_codes = [keep.tile([P, TOKENS], U32, name="a_codes%d" % b, align_bytes=64) for b in range(BATCH)]
-        a_scales = [keep.tile([P, TOKENS], U8, name="a_scales%d" % b, align_bytes=64) for b in range(BATCH)]
+        bias_sb = keep.tile([P, D_OUT], BF16)
 
-        def swish_plane(b, t):
-            nc.vector.scalar_tensor_tensor(
-                out=h_planes[b][:, t, :],
-                in0=plane(xT[b], t),
-                scalar=scale[:, b, t : t + 1],
-                in1=posT_sb[:, t, :],
-                op0=ALU.mult,
-                op1=ALU.add,
-            )
-            nc.scalar.activation(
-                out=a_planes[b][:, t, :],
-                in_=h_planes[b][:, t, :],
-                func=ACT.Silu,
-                bias=shift[:, b, t : t + 1],
-                scale=1.0,
-            )
-
-        def regroup_a(b):
-            regroup(nc.vector.tensor_copy, a_grouped[b][:], a_planes[b][:])
-
-        def quantise_a(b):
-            nc.vector.quantize_mx(
-                out=a_codes[b][:].bitcast(FP8X4),
-                scales=a_scales[b][:],
-                in_=a_grouped[b][:].rearrange("p n t -> p (n t)"),
-            )
-
-        def spread_bias_bank(k, psum, name, copy):
-            bank = psum.tile([P, 2 * N_PASS], BF16, name=name)
+        def spread_bias_bank(k, copy):
+            bank = psum.tile([P, 2 * N_PASS], BF16, name="bank")
             for r in range(BIAS_ROWS_PER_BANK):
                 row = k * BIAS_ROWS_PER_BANK + r
                 nc.tensor.matmul(
@@ -160,113 +139,170 @@ def tile_attentionblock_pa_kernel(tc, x, pos_enc, gamma1, beta1, W_qkv, b_qkv, o
             width = BIAS_ROWS_PER_BANK * BIAS_ROW
             copy(out=bias_sb[:, k * width : (k + 1) * width], in_=bank[:, 0:width])
 
-        stats = keep.tile([P, BATCH * PACK, 6], F32)
-        mean_var = keep.tile([P, BATCH * PACK, 2], F32)
-
-        def transpose_planes(rows_sb, name):
+        def transpose_planes(rows_sb):
             words = rows_sb[:].bitcast(F32)
             banks = []
             for h in range(PACK // 2):
-                bank = head_psum.tile([P, TOKENS], F32, name="%s_%d" % (name, h))
+                bank = psum.tile([P, TOKENS], F32, name="bank")
                 for i in range(TOKEN_TILES):
                     nc.tensor.transpose(bank[:, i * P : (i + 1) * P], words[:, i, h :: PACK // 2], ident[:])
                 banks.append(bank)
             return banks
 
-        def pair(bank):
-            return bank[:].bitcast(BF16).rearrange("p (n e) -> p e n", e=2)
+        def plane(words, t):
+            return words[t // 2][:].bitcast(BF16).rearrange("p (n e) -> p e n", e=2)[:, t % 2, :]
 
-        def plane(banks, t):
-            return pair(banks[t // 2])[:, t % 2, :]
+        xT = {}
+        posT_sb = [keep.tile([P, TOKENS], F32, name="posT_sb%d" % h) for h in range(PACK // 2)]
+        stats = keep.tile([P, BATCH * PACK, 6], F32)
+        mean_var = keep.tile([P, BATCH * PACK, 2], F32)
+        scale = keep.tile([P, BATCH, PACK], F32)
+        shift = keep.tile([P, BATCH, PACK], F32)
+        std = keep.tile([P, BATCH, PACK], F32)
+        rstd = keep.tile([P, BATCH, PACK], F32)
+        mean_scale = keep.tile([P, BATCH, PACK], F32)
+        mean = mean_var[:, :, 0].rearrange("p (b t) -> p b t", b=BATCH)
+        var = mean_var[:, :, 1].rearrange("p (b t) -> p b t", b=BATCH)
+        gamma = gamma_sb[:].unsqueeze(1).to_broadcast([P, BATCH, PACK])
+        beta = beta_sb[:].unsqueeze(1).to_broadcast([P, BATCH, PACK])
 
-        def statistics(b):
+        h_planes = [keep.tile([P, PACK, TOKENS], F32, name="h_planes%d" % b) for b in range(BATCH)]
+        a_planes = [keep.tile([P, PACK, TOKENS], BF16, name="a_planes%d" % b) for b in range(BATCH)]
+        a_grouped = [keep.tile([P, TOKENS, PACK], BF16, name="a_grouped%d" % b, align_bytes=64) for b in range(BATCH)]
+        a_codes = [keep.tile([P, TOKENS], U32, name="a_codes%d" % b, align_bytes=64) for b in range(BATCH)]
+        a_scales = [keep.tile([P, TOKENS], U8, name="a_scales%d" % b, align_bytes=64) for b in range(BATCH)]
+
+        def add_pos(b, t):
+            nc.vector.scalar_tensor_tensor(
+                out=h_planes[b][:, t, :],
+                in0=plane(xT[b], t),
+                scalar=scale[:, b, t : t + 1],
+                in1=plane(posT_sb, t),
+                op0=ALU.mult,
+                op1=ALU.add,
+            )
+
+        def silu(b, t):
+            nc.scalar.activation(
+                out=a_planes[b][:, t, :],
+                in_=h_planes[b][:, t, :],
+                func=ACT.Silu,
+                bias=shift[:, b, t : t + 1],
+                scale=1.0,
+            )
+
+        def regroup_a_half(b, half):
+            tokens = slice(half * HALF_TOKENS, (half + 1) * HALF_TOKENS)
+            interleave(a_grouped[b][:, tokens, :], a_planes[b][:, :, tokens])
+
+        def quantise_a_half(b, half):
+            tokens = slice(half * HALF_TOKENS, (half + 1) * HALF_TOKENS)
+            nc.vector.quantize_mx(
+                out=a_codes[b][:, tokens].bitcast(FP8X4),
+                scales=a_scales[b][:, tokens],
+                in_=a_grouped[b][:, tokens, :].rearrange("p n t -> p (n t)"),
+            )
+
+        xT[0] = transpose_planes(x_sb[0])
+        for k in range(BIAS_BANKS_PER_GROUP):
+            spread_bias_bank(k, nc.scalar.copy)
+        xT[1] = transpose_planes(x_sb[1])
+        posT = transpose_planes(pos_sb)
+        for h in range(PACK // 2):
+            nc.scalar.copy(out=posT_sb[h][:], in_=posT[h][:])
+        for b in range(BATCH):
             for t in range(PACK):
                 nc.vector.bn_stats(out=stats[:, b * PACK + t, :], in_=plane(xT[b], t))
             for t in range(PACK):
                 nc.vector.bn_aggr(out=mean_var[:, b * PACK + t, :], in_=stats[:, b * PACK + t, :])
-
-        with tc.psum_pool(name="head_psum", bufs=1) as head_psum:
-            for k in range(BIAS_BANKS_PER_GROUP):
-                spread_bias_bank(k, head_psum, "bias_bank%d" % k, nc.vector.tensor_copy)
-            for b in range(BATCH):
-                xT[b] = transpose_planes(x_sb[b], "xT%d" % b)
-                statistics(b)
-            posT = transpose_planes(pos_sb, "posT")
-            for h in range(PACK // 2):
-                nc.scalar.copy(out=posT_sb[:, 2 * h : 2 * h + 2, :], in_=pair(posT[h]))
-            for half in range(2):
-                regroup_w_half(PASSES_PER_STORE - 1, half, gpsimd_copy)
-            for half in range(2):
-                regroup_w_half(0, half, nc.vector.tensor_copy)
-
-            std = keep.tile([P, BATCH, PACK], F32)
-            rstd = keep.tile([P, BATCH, PACK], F32)
-            mean_scale = keep.tile([P, BATCH, PACK], F32)
-            mean = mean_var[:, :, 0].rearrange("p (b t) -> p b t", b=BATCH)
-            var = mean_var[:, :, 1].rearrange("p (b t) -> p b t", b=BATCH)
-            gamma = gamma_sb[:].unsqueeze(1).to_broadcast([P, BATCH, PACK])
-            beta = beta_sb[:].unsqueeze(1).to_broadcast([P, BATCH, PACK])
-            nc.scalar.activation(out=std[:], in_=var, func=ACT.Sqrt, bias=EPS, scale=1.0)
-            nc.scalar.activation(out=warm[:, 1:2], in_=std[:, 0, 0:1], func=ACT.Silu)
-            nc.vector.reciprocal(out=rstd[:], in_=std[:])
-            nc.vector.tensor_tensor(out=scale[:], in0=rstd[:], in1=gamma, op=ALU.mult)
-            nc.vector.tensor_tensor(out=mean_scale[:], in0=mean, in1=scale[:], op=ALU.mult)
-            nc.vector.tensor_tensor(out=shift[:], in0=beta, in1=mean_scale[:], op=ALU.subtract)
-
-            for b in range(BATCH):
-                for t in range(PACK):
-                    swish_plane(b, t)
-                if b == 0:
-                    for c in range(1, PASSES_PER_STORE - 1):
-                        for half in range(2):
-                            regroup_w_half(c, half, nc.scalar.copy)
-
-        regroup_a(0)
+        for half in range(2):
+            regroup_w_half(0, half, gpsimd_copy)
+        nc.scalar.activation(out=std[:], in_=var, func=ACT.Sqrt, bias=EPS, scale=1.0)
+        nc.scalar.activation(out=warm[:, 1:2], in_=std[:, 0, 0:1], func=ACT.Silu)
+        nc.vector.reciprocal(out=rstd[:], in_=std[:])
+        nc.vector.tensor_tensor(out=scale[:], in0=rstd[:], in1=gamma, op=ALU.mult)
+        add_pos(0, 0)
+        nc.vector.tensor_tensor(out=mean_scale[:], in0=mean, in1=scale[:], op=ALU.mult)
+        nc.vector.tensor_tensor(out=shift[:], in0=beta, in1=mean_scale[:], op=ALU.subtract)
+        silu(0, 0)
+        for t in range(1, PACK):
+            add_pos(0, t)
+            silu(0, t)
+        for t in range(PACK):
+            add_pos(1, t)
+        for half in range(2):
+            interleave_w_half(1, half)
+        for half in range(2):
+            regroup_a_half(0, half)
+        for half in range(2):
+            interleave_w_half(2, half)
         quantise_w_chunk(0)
-        quantise_a(0)
-        quantise_w_chunk(PASSES_PER_STORE - 1)
-        for c in range(1, PASSES_PER_STORE - 1):
-            quantise_w_chunk(c)
+        quantise_a_half(0, 0)
+        quantise_w_chunk(1)
+        quantise_a_half(0, 1)
+        quantise_w_chunk(2)
 
-        acc_psum = ctx.enter_context(tc.psum_pool(name="acc_psum", bufs=8, reuse_waits="tile"))
-        for g in range(N_GROUPS):
-            for u in range(UNITS):
-                b, i = divmod(u, TOKEN_TILES)
-                tokens = slice(i * P, (i + 1) * P)
-                result = out_stage.tile([P, GROUP], F32)
-                for j in range(PASSES_PER_STORE):
-                    cols = slice(g * GROUP + j * N_PASS, g * GROUP + (j + 1) * N_PASS)
-                    acc = acc_psum.tile([P, N_PASS], F32)
-                    nc.tensor.matmul_mx(
-                        out=acc[:],
-                        lhsT=a_codes[b][:, tokens].bitcast(FP8X4),
-                        lhsT_scale=a_scales[b][:, tokens],
-                        rhs=w_codes[:, cols].bitcast(FP8X4),
-                        rhs_scale=w_scales[:, cols],
-                        start=True,
-                        stop=True,
-                    )
-                    part = result[:, j * N_PASS : (j + 1) * N_PASS]
-                    if ((g * UNITS + u) * PASSES_PER_STORE + j) % SCALAR_SHARE == 0:
-                        nc.scalar.copy(out=part, in_=acc[:])
-                        nc.gpsimd.tensor_tensor(out=part, in0=part, in1=bias_sb[:, cols], op=ALU.add)
-                    else:
-                        nc.vector.tensor_tensor(out=part, in0=acc[:], in1=bias_sb[:, cols], op=ALU.add)
-                nc.sync.dma_start(
-                    out=out[b].rearrange("(m i) n -> i m n", i=TOKEN_TILES)[i, :, g * GROUP : (g + 1) * GROUP],
-                    in_=result[:],
+        behind = {}
+
+        def after(n, *steps):
+            behind.setdefault(n, []).extend(steps)
+
+        def on_scalar(c, half):
+            return lambda: interleave_w_half(c, half) if c < 5 else regroup_w_half(c, half, nc.scalar.copy)
+
+        def quantised(c):
+            return lambda: quantise_w_chunk(c)
+
+        def bias_bank(k):
+            return lambda: spread_bias_bank(k, nc.vector.tensor_copy)
+
+        after(0, lambda: silu(1, 0), lambda: silu(1, 1))
+        after(1, lambda: silu(1, 2), lambda: silu(1, 3))
+        after(2, lambda: regroup_a_half(1, 0), lambda: regroup_a_half(1, 1))
+        after(2, lambda: quantise_a_half(1, 0))
+        after(3, lambda: quantise_a_half(1, 1))
+        after(4, on_scalar(3, 0), on_scalar(3, 1))
+        after(5, on_scalar(4, 0), on_scalar(4, 1), quantised(3))
+        after(5, lambda: regroup_w_half(5, 0, nc.vector.tensor_copy), bias_bank(2))
+        after(6, quantised(4))
+        after(6, lambda: regroup_w_half(5, 1, nc.vector.tensor_copy), bias_bank(3))
+        after(7, quantised(5))
+        for g in range(2, N_GROUPS):
+            first = (g - 1) * UNITS_PER_GROUP
+            for n in range(2 * PASSES_PER_STORE):
+                c = g * PASSES_PER_STORE + n // 2
+                after(first + n, on_scalar(c, n % 2))
+                if n % 2 == 1:
+                    after(first + n + 1, quantised(c))
+            for k in range(BIAS_BANKS_PER_GROUP):
+                after(first + 5 + k, bias_bank(g * BIAS_BANKS_PER_GROUP + k))
+
+        for n in range(N_GROUPS * UNITS_PER_GROUP):
+            g, u = divmod(n, UNITS_PER_GROUP)
+            b, i = divmod(u, TOKEN_TILES)
+            tokens = slice(i * P, (i + 1) * P)
+            result = out_stage.tile([P, GROUP], F32)
+            for j in range(PASSES_PER_STORE):
+                cols = slice(g * GROUP + j * N_PASS, g * GROUP + (j + 1) * N_PASS)
+                acc = psum.tile([P, N_PASS], F32, name="bank")
+                nc.tensor.matmul_mx(
+                    out=acc[:],
+                    lhsT=a_codes[b][:, tokens].bitcast(FP8X4),
+                    lhsT_scale=a_scales[b][:, tokens],
+                    rhs=w_codes[:, cols].bitcast(FP8X4),
+                    rhs_scale=w_scales[:, cols],
+                    start=True,
+                    stop=True,
                 )
-                if g == 0 and b + 1 < BATCH:
-                    if i == 0:
-                        regroup_a(b + 1)
-                    if i == 1:
-                        quantise_a(b + 1)
-                if g + 1 < N_GROUPS and u >= UNITS - BIAS_BANKS_PER_GROUP:
-                    k = (g + 1) * BIAS_BANKS_PER_GROUP + u - (UNITS - BIAS_BANKS_PER_GROUP)
-                    spread_bias_bank(k, acc_psum, "acc", nc.scalar.copy)
-                if g + 1 < N_GROUPS:
-                    next_first = (g + 1) * PASSES_PER_STORE
-                    if u < 2 * PASSES_PER_STORE:
-                        regroup_w_half(next_first + u // 2, u % 2, nc.scalar.copy)
-                    if u >= 2 and u % 2 == 0:
-                        quantise_w_chunk(next_first + u // 2 - 1)
+                part = result[:, j * N_PASS : (j + 1) * N_PASS]
+                if j == 0:
+                    nc.scalar.copy(out=part, in_=acc[:])
+                    nc.gpsimd.tensor_tensor(out=part, in0=part, in1=bias_sb[:, cols], op=ALU.add)
+                else:
+                    nc.vector.tensor_tensor(out=part, in0=acc[:], in1=bias_sb[:, cols], op=ALU.add)
+            nc.sync.dma_start(
+                out=out[b].rearrange("(m i) n -> i m n", i=TOKEN_TILES)[i, :, g * GROUP : (g + 1) * GROUP],
+                in_=result[:],
+            )
+            for step in behind.get(n, []):
+                step()

@@ -54,8 +54,8 @@ def tile_attentionblock_pa_kernel(tc, x, pos_enc, gamma1, beta1, W_qkv, b_qkv, o
         nc.vector.memset(one[:], 1.0)
         bias_rows = keep.tile([P, BIAS_ROW], BF16)
         nc.vector.memset(bias_rows[:], 0.0)
-        ident_bf = keep.tile([P, P], BF16)
-        nc.vector.tensor_copy(out=ident_bf[:], in_=ident[:])
+        ident_bf = keep.tile([P, BIAS_ROWS], BF16)
+        nc.vector.tensor_copy(out=ident_bf[:], in_=ident[:, 0:BIAS_ROWS])
         warm = keep.tile([P, 2], F32)
         nc.scalar.activation(out=warm[:, 0:1], in_=one[:], func=ACT.Sqrt)
 
@@ -92,25 +92,6 @@ def tile_attentionblock_pa_kernel(tc, x, pos_enc, gamma1, beta1, W_qkv, b_qkv, o
                 w_grouped[c][:, first : first + HALF, :],
                 w_raw[g][:, :, j * N_PASS + first : j * N_PASS + first + HALF],
             )
-
-        def interleave(grouped, planes):
-            bank = psum.tile([P, 2 * N_PASS], BF16, name="bank")
-            for q in range(2):
-                nc.tensor.matmul(
-                    bank[:, q * N_PASS : (q + 1) * N_PASS],
-                    lhsT=ident_bf[:],
-                    rhs=planes[:, :, q * P : (q + 1) * P].rearrange("p t n -> p n t"),
-                    start=True,
-                    stop=True,
-                )
-            nc.scalar.copy(out=grouped.rearrange("p n t -> p (n t)"), in_=bank[:])
-
-        def interleave_w_half(c, half):
-            g, j = divmod(c, PASSES_PER_STORE)
-            if half == 0:
-                w_grouped[c] = w_stage.tile([P, N_PASS, PACK], BF16, name="w_grouped", align_bytes=64)
-            first = j * N_PASS + half * HALF
-            interleave(w_grouped[c][:, half * HALF : (half + 1) * HALF, :], w_raw[g][:, :, first : first + HALF])
 
         def gpsimd_copy(out, in_):
             nc.gpsimd.tensor_scalar(out=out, in0=in_, scalar1=1.0, scalar2=0.0, op0=ALU.mult, op1=ALU.add)
@@ -193,7 +174,7 @@ def tile_attentionblock_pa_kernel(tc, x, pos_enc, gamma1, beta1, W_qkv, b_qkv, o
 
         def regroup_a_half(b, half):
             tokens = slice(half * HALF_TOKENS, (half + 1) * HALF_TOKENS)
-            interleave(a_grouped[b][:, tokens, :], a_planes[b][:, :, tokens])
+            regroup(nc.vector.tensor_copy, a_grouped[b][:, tokens, :], a_planes[b][:, :, tokens])
 
         def quantise_a_half(b, half):
             tokens = slice(half * HALF_TOKENS, (half + 1) * HALF_TOKENS)
@@ -231,13 +212,13 @@ def tile_attentionblock_pa_kernel(tc, x, pos_enc, gamma1, beta1, W_qkv, b_qkv, o
         for t in range(PACK):
             add_pos(1, t)
         for half in range(2):
-            interleave_w_half(1, half)
+            regroup_w_half(1, half, nc.scalar.copy)
         for half in range(2):
-            regroup_a_half(0, half)
-        for half in range(2):
-            interleave_w_half(2, half)
+            regroup_w_half(2, half, nc.scalar.copy)
+        regroup_a_half(0, 0)
         quantise_w_chunk(0)
         quantise_a_half(0, 0)
+        regroup_a_half(0, 1)
         quantise_w_chunk(1)
         quantise_a_half(0, 1)
         quantise_w_chunk(2)
@@ -248,7 +229,7 @@ def tile_attentionblock_pa_kernel(tc, x, pos_enc, gamma1, beta1, W_qkv, b_qkv, o
             behind.setdefault(n, []).extend(steps)
 
         def on_scalar(c, half):
-            return lambda: interleave_w_half(c, half) if c < 5 else regroup_w_half(c, half, nc.scalar.copy)
+            return lambda: regroup_w_half(c, half, nc.scalar.copy)
 
         def quantised(c):
             return lambda: quantise_w_chunk(c)
@@ -261,11 +242,12 @@ def tile_attentionblock_pa_kernel(tc, x, pos_enc, gamma1, beta1, W_qkv, b_qkv, o
         after(2, lambda: regroup_a_half(1, 0), lambda: regroup_a_half(1, 1))
         after(2, lambda: quantise_a_half(1, 0))
         after(3, lambda: quantise_a_half(1, 1))
-        after(4, on_scalar(3, 0), on_scalar(3, 1))
-        after(5, on_scalar(4, 0), on_scalar(4, 1), quantised(3))
-        after(5, lambda: regroup_w_half(5, 0, nc.vector.tensor_copy), bias_bank(2))
-        after(6, quantised(4))
-        after(6, lambda: regroup_w_half(5, 1, nc.vector.tensor_copy), bias_bank(3))
+        after(1, on_scalar(3, 0))
+        after(2, on_scalar(3, 1))
+        after(3, on_scalar(4, 0), quantised(3))
+        after(4, on_scalar(4, 1))
+        after(5, on_scalar(5, 0), bias_bank(2), quantised(4))
+        after(6, on_scalar(5, 1), bias_bank(3))
         after(7, quantised(5))
         for g in range(2, N_GROUPS):
             first = (g - 1) * UNITS_PER_GROUP

@@ -27,6 +27,7 @@ BIAS_ROWS = 16
 BIAS_ROW = D_OUT // BIAS_ROWS
 BIAS_ROWS_PER_BANK = 2
 BIAS_BANKS_PER_GROUP = GROUP // (BIAS_ROWS_PER_BANK * BIAS_ROW)
+WARM_UP = 9
 RUN = 4
 
 FLOPS = 2 * BATCH * TOKENS * D_IN * D_OUT
@@ -63,35 +64,33 @@ def tile_attentionblock_pa_kernel(tc, x, pos_enc, gamma1, beta1, W_qkv, b_qkv, o
         pos_sb = keep.tile([P, TOKEN_TILES, D_IN], BF16)
         gamma_sb = keep.tile([P, PACK], BF16)
         beta_sb = keep.tile([P, PACK], BF16)
-        w_raw = [keep.tile([P, PACK, GROUP], BF16, name="w_raw%d" % g) for g in range(N_GROUPS)]
+        w_first = keep.tile([P, PACK, GROUP], BF16)
+        w_rest = keep.tile([P, PACK, D_OUT - GROUP], BF16)
         w_planes = W_qkv.rearrange("(p t) n -> p t n", t=PACK)
 
         def load_tokens(rows_sb, rows):
             nc.sync.dma_start(out=rows_sb[:], in_=rows.rearrange("(m i) d -> m i d", i=TOKEN_TILES))
 
-        load_tokens(x_sb[0], x[0])
+        for h in range(2):
+            nc.sync.dma_start(out=x_sb[0][:, 2 * h : 2 * h + 2, :], in_=x[0].rearrange("(m i) d -> m i d", i=TOKEN_TILES)[:, 2 * h : 2 * h + 2, :])
         nc.sync.dma_start(out=bias_rows[0:BIAS_ROWS, :], in_=b_qkv.rearrange("(r n) -> r n", n=BIAS_ROW))
         nc.sync.dma_start(out=gamma_sb[:], in_=gamma1.rearrange("a b (p t) -> (a b p) t", t=PACK))
         nc.sync.dma_start(out=beta_sb[:], in_=beta1.rearrange("a b (p t) -> (a b p) t", t=PACK))
         load_tokens(x_sb[1], x[1])
         load_tokens(pos_sb, pos_enc[0])
-        for g in range(N_GROUPS):
-            nc.sync.dma_start(out=w_raw[g][:], in_=w_planes[:, :, g * GROUP : (g + 1) * GROUP])
+        nc.sync.dma_start(out=w_first[:], in_=w_planes[:, :, 0:GROUP])
+        nc.sync.dma_start(out=w_rest[:], in_=w_planes[:, :, GROUP:D_OUT])
 
         w_codes = keep.tile([P, D_OUT], U32, align_bytes=64)
         w_scales = keep.tile([P, D_OUT], U8, align_bytes=64)
         w_grouped = {}
 
         def regroup_w_half(c, half, copy):
-            g, j = divmod(c, PASSES_PER_STORE)
             if half == 0:
                 w_grouped[c] = w_stage.tile([P, N_PASS, PACK], BF16, name="w_grouped", align_bytes=64)
-            first = half * HALF
-            regroup(
-                copy,
-                w_grouped[c][:, first : first + HALF, :],
-                w_raw[g][:, :, j * N_PASS + first : j * N_PASS + first + HALF],
-            )
+            raw, first = (w_first, c * N_PASS) if c < PASSES_PER_STORE else (w_rest, c * N_PASS - GROUP)
+            first += half * HALF
+            regroup(copy, w_grouped[c][:, half * HALF : (half + 1) * HALF, :], raw[:, :, first : first + HALF])
 
         def gpsimd_copy(out, in_):
             nc.gpsimd.tensor_scalar(out=out, in0=in_, scalar1=1.0, scalar2=0.0, op0=ALU.mult, op1=ALU.add)
@@ -120,14 +119,19 @@ def tile_attentionblock_pa_kernel(tc, x, pos_enc, gamma1, beta1, W_qkv, b_qkv, o
             width = BIAS_ROWS_PER_BANK * BIAS_ROW
             copy(out=bias_sb[:, k * width : (k + 1) * width], in_=bank[:, 0:width])
 
-        def transpose_planes(rows_sb):
+        def transpose_planes(rows_sb, parts=1, warm_up=0):
             words = rows_sb[:].bitcast(F32)
             banks = []
             for h in range(PACK // 2):
                 bank = psum.tile([P, TOKENS], F32, name="bank")
-                for i in range(TOKEN_TILES):
-                    nc.tensor.transpose(bank[:, i * P : (i + 1) * P], words[:, i, h :: PACK // 2], ident[:])
                 banks.append(bank)
+            for n in range(warm_up):
+                spot = n % TOKEN_TILES
+                nc.tensor.transpose(banks[n // TOKEN_TILES % 2][:, spot * P : (spot + 1) * P], ident[:], ident[:])
+            for i0 in range(0, TOKEN_TILES, TOKEN_TILES // parts):
+                for h in range(PACK // 2):
+                    for i in range(i0, i0 + TOKEN_TILES // parts):
+                        nc.tensor.transpose(banks[h][:, i * P : (i + 1) * P], words[:, i, h :: PACK // 2], ident[:])
             return banks
 
         def plane(words, t):
@@ -184,10 +188,12 @@ def tile_attentionblock_pa_kernel(tc, x, pos_enc, gamma1, beta1, W_qkv, b_qkv, o
                 in_=a_grouped[b][:, tokens, :].rearrange("p n t -> p (n t)"),
             )
 
-        xT[0] = transpose_planes(x_sb[0])
+        xT[0] = transpose_planes(x_sb[0], 2, WARM_UP)
         for k in range(BIAS_BANKS_PER_GROUP):
             spread_bias_bank(k, nc.scalar.copy)
         xT[1] = transpose_planes(x_sb[1])
+        for k in range(BIAS_BANKS_PER_GROUP, 2 * BIAS_BANKS_PER_GROUP):
+            spread_bias_bank(k, nc.scalar.copy)
         posT = transpose_planes(pos_sb)
         for h in range(PACK // 2):
             nc.scalar.copy(out=posT_sb[h][:], in_=posT[h][:])
@@ -237,17 +243,16 @@ def tile_attentionblock_pa_kernel(tc, x, pos_enc, gamma1, beta1, W_qkv, b_qkv, o
         def bias_bank(k):
             return lambda: spread_bias_bank(k, nc.vector.tensor_copy)
 
-        after(0, lambda: silu(1, 0), lambda: silu(1, 1))
-        after(1, lambda: silu(1, 2), lambda: silu(1, 3))
-        after(2, lambda: regroup_a_half(1, 0), lambda: regroup_a_half(1, 1))
-        after(2, lambda: quantise_a_half(1, 0))
+        after(0, lambda: silu(1, 0), lambda: silu(1, 1), lambda: silu(1, 2), lambda: silu(1, 3))
+        after(1, lambda: regroup_a_half(1, 0))
+        after(2, lambda: quantise_a_half(1, 0), lambda: regroup_a_half(1, 1))
         after(3, lambda: quantise_a_half(1, 1))
         after(1, on_scalar(3, 0))
         after(2, on_scalar(3, 1))
         after(3, on_scalar(4, 0), quantised(3))
         after(4, on_scalar(4, 1))
-        after(5, on_scalar(5, 0), bias_bank(2), quantised(4))
-        after(6, on_scalar(5, 1), bias_bank(3))
+        after(5, on_scalar(5, 0), quantised(4))
+        after(6, on_scalar(5, 1))
         after(7, quantised(5))
         for g in range(2, N_GROUPS):
             first = (g - 1) * UNITS_PER_GROUP
@@ -257,7 +262,7 @@ def tile_attentionblock_pa_kernel(tc, x, pos_enc, gamma1, beta1, W_qkv, b_qkv, o
                 if n % 2 == 1:
                     after(first + n + 1, quantised(c))
             for k in range(BIAS_BANKS_PER_GROUP):
-                after(first + 5 + k, bias_bank(g * BIAS_BANKS_PER_GROUP + k))
+                after(first + 3 + 4 * k, bias_bank(g * BIAS_BANKS_PER_GROUP + k))
 
         for n in range(N_GROUPS * UNITS_PER_GROUP):
             g, u = divmod(n, UNITS_PER_GROUP)
@@ -277,7 +282,7 @@ def tile_attentionblock_pa_kernel(tc, x, pos_enc, gamma1, beta1, W_qkv, b_qkv, o
                     stop=True,
                 )
                 part = result[:, j * N_PASS : (j + 1) * N_PASS]
-                if j == 0:
+                if j == 0 and n > 0:
                     nc.scalar.copy(out=part, in_=acc[:])
                     nc.gpsimd.tensor_tensor(out=part, in0=part, in1=bias_sb[:, cols], op=ALU.add)
                 else:

from contextlib import ExitStack

import concourse.mybir as mybir
from concourse.masks import make_identity

F32 = mybir.dt.float32
BF16 = mybir.dt.bfloat16
U32 = mybir.dt.uint32
U8 = mybir.dt.uint8
FP8X4 = mybir.dt.float8_e4m3fn_x4
ALU = mybir.AluOpType
ACT = mybir.ActivationFunctionType

P = 128
PACK = 4
BATCH, TOKENS, D_IN, D_OUT = 2, 512, 512, 6144
EPS = 1e-5
TOKEN_TILES = TOKENS // P
N_PASS = 512
HALF = N_PASS // 2
PASSES_PER_STORE = 3
GROUP = N_PASS * PASSES_PER_STORE
N_GROUPS = D_OUT // GROUP
UNITS_PER_GROUP = BATCH * TOKEN_TILES
HALF_TOKENS = TOKENS // 2
BIAS_ROWS = 16
BIAS_ROW = D_OUT // BIAS_ROWS
BIAS_ROWS_PER_BANK = 2
BIAS_BANKS_PER_GROUP = GROUP // (BIAS_ROWS_PER_BANK * BIAS_ROW)
WARM_UP = 9
RUN = 4

FLOPS = 2 * BATCH * TOKENS * D_IN * D_OUT


def regroup(copy, grouped, planes):
    copy(
        out=grouped.rearrange("p (c i) t -> p c t i", i=RUN),
        in_=planes.rearrange("p t (c i) -> p c t i", i=RUN),
    )


def tile_attentionblock_pa_kernel(tc, x, pos_enc, gamma1, beta1, W_qkv, b_qkv, out):
    nc = tc.nc
    with ExitStack() as ctx:
        ctx.enter_context(tc.manual_schedule())
        keep = ctx.enter_context(tc.tile_pool(name="keep", bufs=1))
        w_stage = ctx.enter_context(tc.tile_pool(name="w_stage", bufs=4))
        out_stage = ctx.enter_context(tc.tile_pool(name="out_stage", bufs=8))
        psum = ctx.enter_context(tc.psum_pool(name="psum", bufs=8, reuse_waits="tile"))

        ident = keep.tile([P, P], F32)
        make_identity(nc, ident[:])
        one = keep.tile([P, 1], F32)
        nc.vector.memset(one[:], 1.0)
        bias_rows = keep.tile([P, BIAS_ROW], BF16)
        nc.vector.memset(bias_rows[:], 0.0)
        ident_bf = keep.tile([P, BIAS_ROWS], BF16)
        nc.vector.tensor_copy(out=ident_bf[:], in_=ident[:, 0:BIAS_ROWS])
        warm = keep.tile([P, 2], F32)
        nc.scalar.activation(out=warm[:, 0:1], in_=one[:], func=ACT.Sqrt)

        x_sb = [keep.tile([P, TOKEN_TILES, D_IN], BF16, name="x_sb%d" % b) for b in range(BATCH)]
        pos_sb = keep.tile([P, TOKEN_TILES, D_IN], BF16)
        gamma_sb = keep.tile([P, PACK], BF16)
        beta_sb = keep.tile([P, PACK], BF16)
        w_first = keep.tile([P, PACK, GROUP], BF16)
        w_rest = keep.tile([P, PACK, D_OUT - GROUP], BF16)
        w_planes = W_qkv.rearrange("(p t) n -> p t n", t=PACK)

        def load_tokens(rows_sb, rows):
            nc.sync.dma_start(out=rows_sb[:], in_=rows.rearrange("(m i) d -> m i d", i=TOKEN_TILES))

        for h in range(2):
            nc.sync.dma_start(out=x_sb[0][:, 2 * h : 2 * h + 2, :], in_=x[0].rearrange("(m i) d -> m i d", i=TOKEN_TILES)[:, 2 * h : 2 * h + 2, :])
        nc.sync.dma_start(out=bias_rows[0:BIAS_ROWS, :], in_=b_qkv.rearrange("(r n) -> r n", n=BIAS_ROW))
        nc.sync.dma_start(out=gamma_sb[:], in_=gamma1.rearrange("a b (p t) -> (a b p) t", t=PACK))
        nc.sync.dma_start(out=beta_sb[:], in_=beta1.rearrange("a b (p t) -> (a b p) t", t=PACK))
        load_tokens(x_sb[1], x[1])
        load_tokens(pos_sb, pos_enc[0])
        nc.sync.dma_start(out=w_first[:], in_=w_planes[:, :, 0:GROUP])
        nc.sync.dma_start(out=w_rest[:], in_=w_planes[:, :, GROUP:D_OUT])

        w_codes = keep.tile([P, D_OUT], U32, align_bytes=64)
        w_scales = keep.tile([P, D_OUT], U8, align_bytes=64)
        w_grouped = {}

        def regroup_w_half(c, half, copy):
            if half == 0:
                w_grouped[c] = w_stage.tile([P, N_PASS, PACK], BF16, name="w_grouped", align_bytes=64)
            raw, first = (w_first, c * N_PASS) if c < PASSES_PER_STORE else (w_rest, c * N_PASS - GROUP)
            first += half * HALF
            regroup(copy, w_grouped[c][:, half * HALF : (half + 1) * HALF, :], raw[:, :, first : first + HALF])

        def gpsimd_copy(out, in_):
            nc.gpsimd.tensor_scalar(out=out, in0=in_, scalar1=1.0, scalar2=0.0, op0=ALU.mult, op1=ALU.add)

        def quantise_w_chunk(c):
            cols = slice(c * N_PASS, (c + 1) * N_PASS)
            nc.vector.quantize_mx(
                out=w_codes[:, cols].bitcast(FP8X4),
                scales=w_scales[:, cols],
                in_=w_grouped[c][:].rearrange("p n t -> p (n t)"),
            )

        bias_sb = keep.tile([P, D_OUT], BF16)

        def spread_bias_bank(k, copy):
            bank = psum.tile([P, 2 * N_PASS], BF16, name="bank")
            for r in range(BIAS_ROWS_PER_BANK):
                row = k * BIAS_ROWS_PER_BANK + r
                nc.tensor.matmul(
                    bank[:, r * BIAS_ROW : (r + 1) * BIAS_ROW],
                    lhsT=ident_bf[:, row : row + 1].to_broadcast([P, P]),
                    rhs=bias_rows[:],
                    start=True,
                    stop=True,
                )
            width = BIAS_ROWS_PER_BANK * BIAS_ROW
            copy(out=bias_sb[:, k * width : (k + 1) * width], in_=bank[:, 0:width])

        def transpose_planes(rows_sb, parts=1, warm_up=0):
            words = rows_sb[:].bitcast(F32)
            banks = []
            for h in range(PACK // 2):
                bank = psum.tile([P, TOKENS], F32, name="bank")
                banks.append(bank)
            for n in range(warm_up):
                spot = n % TOKEN_TILES
                nc.tensor.transpose(banks[n // TOKEN_TILES % 2][:, spot * P : (spot + 1) * P], ident[:], ident[:])
            for i0 in range(0, TOKEN_TILES, TOKEN_TILES // parts):
                for h in range(PACK // 2):
                    for i in range(i0, i0 + TOKEN_TILES // parts):
                        nc.tensor.transpose(banks[h][:, i * P : (i + 1) * P], words[:, i, h :: PACK // 2], ident[:])
            return banks

        def plane(words, t):
            return words[t // 2][:].bitcast(BF16).rearrange("p (n e) -> p e n", e=2)[:, t % 2, :]

        xT = {}
        posT_sb = [keep.tile([P, TOKENS], F32, name="posT_sb%d" % h) for h in range(PACK // 2)]
        stats = keep.tile([P, BATCH * PACK, 6], F32)
        mean_var = keep.tile([P, BATCH * PACK, 2], F32)
        scale = keep.tile([P, BATCH, PACK], F32)
        shift = keep.tile([P, BATCH, PACK], F32)
        std = keep.tile([P, BATCH, PACK], F32)
        rstd = keep.tile([P, BATCH, PACK], F32)
        mean_scale = keep.tile([P, BATCH, PACK], F32)
        mean = mean_var[:, :, 0].rearrange("p (b t) -> p b t", b=BATCH)
        var = mean_var[:, :, 1].rearrange("p (b t) -> p b t", b=BATCH)
        gamma = gamma_sb[:].unsqueeze(1).to_broadcast([P, BATCH, PACK])
        beta = beta_sb[:].unsqueeze(1).to_broadcast([P, BATCH, PACK])

        h_planes = [keep.tile([P, PACK, TOKENS], F32, name="h_planes%d" % b) for b in range(BATCH)]
        a_planes = [keep.tile([P, PACK, TOKENS], BF16, name="a_planes%d" % b) for b in range(BATCH)]
        a_grouped = [keep.tile([P, TOKENS, PACK], BF16, name="a_grouped%d" % b, align_bytes=64) for b in range(BATCH)]
        a_codes = [keep.tile([P, TOKENS], U32, name="a_codes%d" % b, align_bytes=64) for b in range(BATCH)]
        a_scales = [keep.tile([P, TOKENS], U8, name="a_scales%d" % b, align_bytes=64) for b in range(BATCH)]

        def add_pos(b, t):
            nc.vector.scalar_tensor_tensor(
                out=h_planes[b][:, t, :],
                in0=plane(xT[b], t),
                scalar=scale[:, b, t : t + 1],
                in1=plane(posT_sb, t),
                op0=ALU.mult,
                op1=ALU.add,
            )

        def silu(b, t):
            nc.scalar.activation(
                out=a_planes[b][:, t, :],
                in_=h_planes[b][:, t, :],
                func=ACT.Silu,
                bias=shift[:, b, t : t + 1],
                scale=1.0,
            )

        def regroup_a_half(b, half):
            tokens = slice(half * HALF_TOKENS, (half + 1) * HALF_TOKENS)
            regroup(nc.vector.tensor_copy, a_grouped[b][:, tokens, :], a_planes[b][:, :, tokens])

        def quantise_a_half(b, half):
            tokens = slice(half * HALF_TOKENS, (half + 1) * HALF_TOKENS)
            nc.vector.quantize_mx(
                out=a_codes[b][:, tokens].bitcast(FP8X4),
                scales=a_scales[b][:, tokens],
                in_=a_grouped[b][:, tokens, :].rearrange("p n t -> p (n t)"),
            )

        xT[0] = transpose_planes(x_sb[0], 2, WARM_UP)
        for k in range(BIAS_BANKS_PER_GROUP):
            spread_bias_bank(k, nc.scalar.copy)
        xT[1] = transpose_planes(x_sb[1])
        for k in range(BIAS_BANKS_PER_GROUP, 2 * BIAS_BANKS_PER_GROUP):
            spread_bias_bank(k, nc.scalar.copy)
        posT = transpose_planes(pos_sb)
        for h in range(PACK // 2):
            nc.scalar.copy(out=posT_sb[h][:], in_=posT[h][:])
        for b in range(BATCH):
            for t in range(PACK):
                nc.vector.bn_stats(out=stats[:, b * PACK + t, :], in_=plane(xT[b], t))
            for t in range(PACK):
                nc.vector.bn_aggr(out=mean_var[:, b * PACK + t, :], in_=stats[:, b * PACK + t, :])
        for half in range(2):
            regroup_w_half(0, half, gpsimd_copy)
        nc.scalar.activation(out=std[:], in_=var, func=ACT.Sqrt, bias=EPS, scale=1.0)
        nc.scalar.activation(out=warm[:, 1:2], in_=std[:, 0, 0:1], func=ACT.Silu)
        nc.vector.reciprocal(out=rstd[:], in_=std[:])
        nc.vector.tensor_tensor(out=scale[:], in0=rstd[:], in1=gamma, op=ALU.mult)
        add_pos(0, 0)
        nc.vector.tensor_tensor(out=mean_scale[:], in0=mean, in1=scale[:], op=ALU.mult)
        nc.vector.tensor_tensor(out=shift[:], in0=beta, in1=mean_scale[:], op=ALU.subtract)
        silu(0, 0)
        for t in range(1, PACK):
            add_pos(0, t)
            silu(0, t)
        for t in range(PACK):
            add_pos(1, t)
        for half in range(2):
            regroup_w_half(1, half, nc.scalar.copy)
        for half in range(2):
            regroup_w_half(2, half, nc.scalar.copy)
        regroup_a_half(0, 0)
        quantise_w_chunk(0)
        quantise_a_half(0, 0)
        regroup_a_half(0, 1)
        quantise_w_chunk(1)
        quantise_a_half(0, 1)
        quantise_w_chunk(2)

        behind = {}

        def after(n, *steps):
            behind.setdefault(n, []).extend(steps)

        def on_scalar(c, half):
            return lambda: regroup_w_half(c, half, nc.scalar.copy)

        def quantised(c):
            return lambda: quantise_w_chunk(c)

        def bias_bank(k):
            return lambda: spread_bias_bank(k, nc.vector.tensor_copy)

        after(0, lambda: silu(1, 0), lambda: silu(1, 1), lambda: silu(1, 2), lambda: silu(1, 3))
        after(1, lambda: regroup_a_half(1, 0))
        after(2, lambda: quantise_a_half(1, 0), lambda: regroup_a_half(1, 1))
        after(3, lambda: quantise_a_half(1, 1))
        after(1, on_scalar(3, 0))
        after(2, on_scalar(3, 1))
        after(3, on_scalar(4, 0), quantised(3))
        after(4, on_scalar(4, 1))
        after(5, on_scalar(5, 0), quantised(4))
        after(6, on_scalar(5, 1))
        after(7, quantised(5))
        for g in range(2, N_GROUPS):
            first = (g - 1) * UNITS_PER_GROUP
            for n in range(2 * PASSES_PER_STORE):
                c = g * PASSES_PER_STORE + n // 2
                after(first + n, on_scalar(c, n % 2))
                if n % 2 == 1:
                    after(first + n + 1, quantised(c))
            for k in range(BIAS_BANKS_PER_GROUP):
                after(first + 3 + 4 * k, bias_bank(g * BIAS_BANKS_PER_GROUP + k))

        for n in range(N_GROUPS * UNITS_PER_GROUP):
            g, u = divmod(n, UNITS_PER_GROUP)
            b, i = divmod(u, TOKEN_TILES)
            tokens = slice(i * P, (i + 1) * P)
            result = out_stage.tile([P, GROUP], F32)
            for j in range(PASSES_PER_STORE):
                cols = slice(g * GROUP + j * N_PASS, g * GROUP + (j + 1) * N_PASS)
                acc = psum.tile([P, N_PASS], F32, name="bank")
                nc.tensor.matmul_mx(
                    out=acc[:],
                    lhsT=a_codes[b][:, tokens].bitcast(FP8X4),
                    lhsT_scale=a_scales[b][:, tokens],
                    rhs=w_codes[:, cols].bitcast(FP8X4),
                    rhs_scale=w_scales[:, cols],
                    start=True,
                    stop=True,
                )
                part = result[:, j * N_PASS : (j + 1) * N_PASS]
                if j == 0 and n > 0:
                    nc.scalar.copy(out=part, in_=acc[:])
                    nc.gpsimd.tensor_tensor(out=part, in0=part, in1=bias_sb[:, cols], op=ALU.add)
                else:
                    nc.vector.tensor_tensor(out=part, in0=acc[:], in1=bias_sb[:, cols], op=ALU.add)
            nc.sync.dma_start(
                out=out[b].rearrange("(m i) n -> i m n", i=TOKEN_TILES)[i, :, g * GROUP : (g + 1) * GROUP],
                in_=result[:],
            )
            for step in behind.get(n, []):
                step()
